import numpy as np
import ml_dtypes


def mxq(x, axis, fmt="e4m3"):
    dtype, down = {"e4m3": (ml_dtypes.float8_e4m3fn, 7), "e5m2": (ml_dtypes.float8_e5m2, 14)}[fmt]
    v = np.moveaxis(np.asarray(x, np.float32).astype(ml_dtypes.bfloat16).astype(np.float64), axis, -1)
    blocks = v.reshape(v.shape[:-1] + (-1, 32))
    amax = np.abs(blocks).max(-1, keepdims=True)
    byte = np.maximum(np.where(amax > 0, np.frexp(amax)[1] - 1 + 127, 0) - down, 1)
    scale = np.exp2(byte - 127.0)
    codes = (blocks / scale).astype(np.float32).astype(dtype).astype(np.float64)
    return np.moveaxis((codes * scale).reshape(v.shape), -1, axis)


WIDE = False


def mx_kscale(k):
    if not WIDE:
        return np.ones(k)
    levels = np.array([10, -10, 5, -5, 0])
    a = np.random.permutation(np.resize(levels, k // 512 * 4)).reshape(k // 512, 4)
    idx = np.arange(k)
    return np.exp2(a[idx // 512, idx % 128 // 32])


BF16 = ml_dtypes.bfloat16


def bf(x):
    return np.asarray(x, np.float32).astype(BF16)


def f64(x):
    return np.asarray(x).astype(np.float64)


NB, C, O, CZ, DD, HH, WW, MG = 1, 512, 512, 512, 4, 8, 16, 4
STRIDES = (2, 2, 2)


def setup_inputs():
    s = mx_kscale(C)
    sd, sh, sw = STRIDES
    return {"x": bf(np.random.standard_normal((NB, C, DD, HH, WW)) * s[None, :, None, None, None]),
            "z": bf(np.random.standard_normal((NB, CZ, sd * DD + MG, sh * HH + MG, sw * WW + MG))),
            "W": bf(np.random.standard_normal((O, C)) / np.sqrt(C) / s[None, :]),
            "b": bf(np.random.standard_normal(O) * 0.5)}


def reference(x, z, W, b):
    sd, sh, sw = STRIDES
    u = np.repeat(np.repeat(np.repeat(f64(x), sd, axis=2), sh, axis=3), sw, axis=4)
    n, c, d, h, w = u.shape
    y = mxq(f64(W), 1, "e4m3") @ mxq(u.reshape(n, c, d * h * w), 1, "e4m3")
    y = y.reshape(n, -1, d, h, w) + f64(b)[None, :, None, None, None]
    zf = f64(z)
    off = [(zf.shape[i] - y.shape[i]) // 2 for i in range(2, 5)]
    zc = zf[:, :,
            off[0]:off[0] + y.shape[2],
            off[1]:off[1] + y.shape[3],
            off[2]:off[2] + y.shape[4]]
    return np.concatenate([y, zc], axis=1)

@@ -1,0 +1,131 @@
+from contextlib import ExitStack
+
+import concourse.mybir as mybir
+from concourse.masks import make_identity
+
+FP8X4 = mybir.dt.float8_e4m3fn_x4
+BF16 = mybir.dt.bfloat16
+F32 = mybir.dt.float32
+U32 = mybir.dt.uint32
+U8 = mybir.dt.uint8
+
+P = 128
+PACK = 4
+C = 512
+O = 512
+CZ = 512
+XD, XH, XW = 4, 8, 16
+X_POS = XD * XH * XW
+YD, YH, YW = 8, 16, 32
+Y_POS = YD * YH * YW
+ZH, ZW = 20, 36
+MARGIN = 2
+GROUPS = 4
+N_PASS = 512
+
+FLOPS = 2 * O * C * Y_POS
+BYTES = 2 * (C * X_POS + O * C + O + CZ * Y_POS) + 4 * (O + CZ) * Y_POS
+
+
+def tile_upconvcropcat_kernel(tc, x, z, W, b, out):
+    nc = tc.nc
+    with ExitStack() as ctx:
+        keep = ctx.enter_context(tc.tile_pool(name="keep", bufs=1))
+        psum_w = ctx.enter_context(tc.psum_pool(name="psum_w", bufs=2))
+        psum_y = ctx.enter_context(tc.psum_pool(name="psum_y", bufs=6))
+
+        out_rows = out[0].rearrange("c d h w -> c (d h w)")
+        y_dram = out_rows[0:O, :].rearrange("(p m) n -> p m n", m=GROUPS)
+        zc_dram = out_rows[O : O + CZ, :].rearrange("(p g) n -> p g n", g=GROUPS)
+        z_dram = z[0].rearrange("(p g) d h w -> p g d h w", g=GROUPS)
+
+        x_sb = keep.tile([P, PACK, X_POS], BF16)
+        nc.sync.dma_start(out=x_sb[:], in_=x[0].rearrange("(p t) d h w -> p t (d h w)", t=PACK))
+        w_sb = keep.tile([P, GROUPS * C], BF16)
+        nc.sync.dma_start(out=w_sb[:], in_=W.rearrange("(p m) c -> p (m c)", m=GROUPS))
+        b_sb = keep.tile([P, GROUPS], BF16)
+        nc.scalar.dma_start(out=b_sb[:], in_=b.rearrange("(p m) -> p m", m=GROUPS))
+        z_in = []
+        for g in range(GROUPS):
+            z_g = keep.tile([P, YD, ZH, ZW], BF16, name="z_in%d" % g)
+            nc.sync.dma_start(out=z_g[:], in_=z_dram[:, g, MARGIN : MARGIN + YD, :, :])
+            z_in.append(z_g)
+
+        ident = keep.tile([P, P], F32)
+        make_identity(nc, ident[:])
+
+        u_bf = keep.tile([P, 2 * X_POS * PACK], BF16, align_bytes=64)
+        u_codes = keep.tile([P, 2 * X_POS], U32, align_bytes=64)
+        u_scales = keep.tile([P, 2 * X_POS], U8, align_bytes=64)
+        half_pos = X_POS // 2
+        for h in range(2):
+            nc.vector.tensor_copy(
+                out=u_bf[:, h * N_PASS * PACK : (h + 1) * N_PASS * PACK].rearrange(
+                    "p (n r t) -> p n r t", r=2, t=PACK
+                ),
+                in_=x_sb[:, :, h * half_pos : (h + 1) * half_pos]
+                .rearrange("p t n -> p n t")
+                .unsqueeze(2)
+                .to_broadcast([P, half_pos, 2, PACK]),
+            )
+
+        w_words = w_sb[:].bitcast(F32).rearrange("p (m q u) -> p m u q", m=GROUPS, u=2)
+        w_bf = keep.tile([P, GROUPS * P * PACK], BF16, align_bytes=64)
+        w_bf_words = w_bf[:].bitcast(F32).rearrange("q (m p u) -> q m p u", m=GROUPS, u=2)
+        w_codes = keep.tile([P, GROUPS * P], U32, align_bytes=64)
+        w_scales = keep.tile([P, GROUPS * P], U8, align_bytes=64)
+        for mp in range(2):
+            w_t = psum_w.tile([P, 2, 2, P], F32, name="w_t")
+            for mm in range(2):
+                for u in range(2):
+                    nc.tensor.transpose(w_t[:, mm, u, :], w_words[:, 2 * mp + mm, u, :], ident[:])
+            nc.vector.tensor_copy(
+                out=w_bf_words[:, 2 * mp : 2 * mp + 2, :, :],
+                in_=w_t[:].rearrange("q mm u p -> q mm p u"),
+            )
+
+        for h in range(2):
+            nc.vector.quantize_mx(
+                out=u_codes[:, h * N_PASS : (h + 1) * N_PASS].bitcast(FP8X4),
+                scales=u_scales[:, h * N_PASS : (h + 1) * N_PASS],
+                in_=u_bf[:, h * N_PASS * PACK : (h + 1) * N_PASS * PACK],
+            )
+        nc.vector.quantize_mx(out=w_codes[:].bitcast(FP8X4), scales=w_scales[:], in_=w_bf[:])
+
+        bias = keep.tile([P, GROUPS], F32)
+        nc.vector.tensor_copy(out=bias[:], in_=b_sb[:])
+
+        y_sb = keep.tile([P, GROUPS, Y_POS], F32)
+        y_view = y_sb[:].rearrange(
+            "p m (ip ii di j dj k) -> p m ip ii di j dj k", ip=2, ii=2, di=2, j=XH, dj=2
+        )
+        zc_sb = keep.tile([P, GROUPS, Y_POS], F32)
+        for g in range(GROUPS):
+            nc.vector.tensor_copy(
+                out=zc_sb[:, g, :].rearrange("p (d h w) -> p d h w", d=YD, h=YH),
+                in_=z_in[g][:, :, MARGIN : MARGIN + YH, MARGIN : MARGIN + YW],
+            )
+            nc.sync.dma_start(out=zc_dram[:, g, :], in_=zc_sb[:, g, :])
+
+            m = g
+            for ip in range(2):
+                for di in range(2):
+                    for dj in range(2):
+                        acc = psum_y.tile([P, N_PASS], F32, name="acc")
+                        nc.tensor.matmul_mx(
+                            out=acc[:],
+                            lhsT=w_codes[:, m * P : (m + 1) * P].bitcast(FP8X4),
+                            lhsT_scale=w_scales[:, m * P : (m + 1) * P],
+                            rhs=u_codes[:, ip * N_PASS : (ip + 1) * N_PASS].bitcast(FP8X4),
+                            rhs_scale=u_scales[:, ip * N_PASS : (ip + 1) * N_PASS],
+                            start=True,
+                            stop=True,
+                        )
+                        nc.scalar.activation(
+                            out=y_view[:, m, ip, :, di, :, dj, :],
+                            in_=acc[:].rearrange("p (ii j k) -> p ii j k", ii=2, j=XH),
+                            func=mybir.ActivationFunctionType.Identity,
+                            bias=bias[:, m : m + 1],
+                            scale=1.0,
+                        )
+            nc.sync.dma_start(out=y_dram[:, m, :], in_=y_sb[:, m, :])

@@ -47,8 +47,8 @@ def tile_upconvcropcat_kernel(tc, x, z, W, b, out):
         nc.scalar.dma_start(out=b_sb[:], in_=b.rearrange("(p m) -> p m", m=GROUPS))
         z_in = []
         for g in range(GROUPS):
-            z_g = keep.tile([P, YD, ZH, ZW], BF16, name="z_in%d" % g)
-            nc.sync.dma_start(out=z_g[:], in_=z_dram[:, g, MARGIN : MARGIN + YD, :, :])
+            z_g = keep.tile([P, YD, YH, ZW], BF16, name="z_in%d" % g)
+            nc.sync.dma_start(out=z_g[:], in_=z_dram[:, g, MARGIN : MARGIN + YD, MARGIN : MARGIN + YH, :])
             z_in.append(z_g)
 
         ident = keep.tile([P, P], F32)
@@ -103,7 +103,7 @@ def tile_upconvcropcat_kernel(tc, x, z, W, b, out):
         for g in range(GROUPS):
             nc.vector.tensor_copy(
                 out=zc_sb[:, g, :].rearrange("p (d h w) -> p d h w", d=YD, h=YH),
-                in_=z_in[g][:, :, MARGIN : MARGIN + YH, MARGIN : MARGIN + YW],
+                in_=z_in[g][:, :, :, MARGIN : MARGIN + YW],
             )
             nc.sync.dma_start(out=zc_dram[:, g, :], in_=zc_sb[:, g, :])
 

@@ -21,6 +21,12 @@ Y_POS = YD * YH * YW
 ZH, ZW = 20, 36
 MARGIN = 2
 GROUPS = 4
+Z_CH = 12 * ZH * ZW
+Z_NEED_FIRST = (MARGIN * ZH + MARGIN) * ZW + MARGIN
+Z_NEED_LAST = ((MARGIN + YD - 1) * ZH + MARGIN + YH - 1) * ZW + MARGIN + YW - 1
+Z_LO = Z_NEED_FIRST // 32 * 32
+Z_HI = (Z_NEED_LAST + 32) // 32 * 32
+Z_SKIP = Z_NEED_FIRST - Z_LO
 N_PASS = 512
 
 FLOPS = 2 * O * C * Y_POS
@@ -37,7 +43,7 @@ def tile_upconvcropcat_kernel(tc, x, z, W, b, out):
         out_rows = out[0].rearrange("c d h w -> c (d h w)")
         y_dram = out_rows[0:O, :].rearrange("(p m) n -> p m n", m=GROUPS)
         zc_dram = out_rows[O : O + CZ, :].rearrange("(p g) n -> p g n", g=GROUPS)
-        z_dram = z[0].rearrange("(p g) d h w -> p g d h w", g=GROUPS)
+        z_dram = z[0].rearrange("(p g) d h w -> p g (d h w)", g=GROUPS)
 
         x_sb = keep.tile([P, PACK, X_POS], BF16)
         nc.sync.dma_start(out=x_sb[:], in_=x[0].rearrange("(p t) d h w -> p t (d h w)", t=PACK))
@@ -47,8 +53,8 @@ def tile_upconvcropcat_kernel(tc, x, z, W, b, out):
         nc.scalar.dma_start(out=b_sb[:], in_=b.rearrange("(p m) -> p m", m=GROUPS))
         z_in = []
         for g in range(GROUPS):
-            z_g = keep.tile([P, YD, YH, ZW], BF16, name="z_in%d" % g)
-            nc.sync.dma_start(out=z_g[:], in_=z_dram[:, g, MARGIN : MARGIN + YD, MARGIN : MARGIN + YH, :])
+            z_g = keep.tile([P, Z_SKIP + YD * ZH * ZW], BF16, name="z_in%d" % g)
+            nc.sync.dma_start(out=z_g[:, 0 : Z_HI - Z_LO], in_=z_dram[:, g, Z_LO:Z_HI])
             z_in.append(z_g)
 
         ident = keep.tile([P, P], F32)
@@ -103,9 +109,14 @@ def tile_upconvcropcat_kernel(tc, x, z, W, b, out):
         for g in range(GROUPS):
             nc.vector.tensor_copy(
                 out=zc_sb[:, g, :].rearrange("p (d h w) -> p d h w", d=YD, h=YH),
-                in_=z_in[g][:, :, :, MARGIN : MARGIN + YW],
+                in_=z_in[g][:, Z_SKIP : Z_SKIP + YD * ZH * ZW]
+                .rearrange("p (d r) -> p d r", d=YD)[:, :, 0 : YH * ZW]
+                .rearrange("p d (h w) -> p d h w", h=YH)[:, :, :, 0:YW],
             )
-            nc.sync.dma_start(out=zc_dram[:, g, :], in_=zc_sb[:, g, :])
+            if g == 0:
+                nc.sync.dma_start(out=zc_dram[:, 0, :], in_=zc_sb[:, 0, :])
+            if g == GROUPS - 1:
+                nc.sync.dma_start(out=zc_dram[:, 1:GROUPS, :], in_=zc_sb[:, 1:GROUPS, :])
 
             m = g
             for ip in range(2):
@@ -121,11 +132,20 @@ def tile_upconvcropcat_kernel(tc, x, z, W, b, out):
                             start=True,
                             stop=True,
                         )
-                        nc.scalar.activation(
-                            out=y_view[:, m, ip, :, di, :, dj, :],
-                            in_=acc[:].rearrange("p (ii j k) -> p ii j k", ii=2, j=XH),
-                            func=mybir.ActivationFunctionType.Identity,
-                            bias=bias[:, m : m + 1],
-                            scale=1.0,
-                        )
-            nc.sync.dma_start(out=y_dram[:, m, :], in_=y_sb[:, m, :])
+                        if m < GROUPS - 1:
+                            nc.scalar.activation(
+                                out=y_view[:, m, ip, :, di, :, dj, :],
+                                in_=acc[:].rearrange("p (ii j k) -> p ii j k", ii=2, j=XH),
+                                func=mybir.ActivationFunctionType.Identity,
+                                bias=bias[:, m : m + 1],
+                                scale=1.0,
+                            )
+                        else:
+                            nc.vector.tensor_scalar(
+                                out=y_view[:, m, ip, :, di, :, dj, :],
+                                in0=acc[:].rearrange("p (ii j k) -> p ii j k", ii=2, j=XH),
+                                scalar1=bias[:, m : m + 1],
+                                scalar2=None,
+                                op0=mybir.AluOpType.add,
+                            )
+        nc.sync.dma_start(out=y_dram, in_=y_sb[:])

@@ -39,6 +39,7 @@ def tile_upconvcropcat_kernel(tc, x, z, W, b, out):
         keep = ctx.enter_context(tc.tile_pool(name="keep", bufs=1))
         psum_w = ctx.enter_context(tc.psum_pool(name="psum_w", bufs=2))
         psum_y = ctx.enter_context(tc.psum_pool(name="psum_y", bufs=6))
+        ctx.enter_context(tc.manual_schedule())
 
         out_rows = out[0].rearrange("c d h w -> c (d h w)")
         y_dram = out_rows[0:O, :].rearrange("(p m) n -> p m n", m=GROUPS)
@@ -48,13 +49,14 @@ def tile_upconvcropcat_kernel(tc, x, z, W, b, out):
         x_sb = keep.tile([P, PACK, X_POS], BF16)
         nc.sync.dma_start(out=x_sb[:], in_=x[0].rearrange("(p t) d h w -> p t (d h w)", t=PACK))
         w_sb = keep.tile([P, GROUPS * C], BF16)
-        nc.sync.dma_start(out=w_sb[:], in_=W.rearrange("(p m) c -> p (m c)", m=GROUPS))
+        nc.scalar.dma_start(out=w_sb[:], in_=W.rearrange("(p m) c -> p (m c)", m=GROUPS))
         b_sb = keep.tile([P, GROUPS], BF16)
         nc.scalar.dma_start(out=b_sb[:], in_=b.rearrange("(p m) -> p m", m=GROUPS))
         z_in = []
         for g in range(GROUPS):
             z_g = keep.tile([P, Z_SKIP + YD * ZH * ZW], BF16, name="z_in%d" % g)
-            nc.sync.dma_start(out=z_g[:, 0 : Z_HI - Z_LO], in_=z_dram[:, g, Z_LO:Z_HI])
+            queue = nc.sync if g % 2 == 0 else nc.scalar
+            queue.dma_start(out=z_g[:, 0 : Z_HI - Z_LO], in_=z_dram[:, g, Z_LO:Z_HI])
             z_in.append(z_g)
 
         ident = keep.tile([P, P], F32)
@@ -85,21 +87,18 @@ def tile_upconvcropcat_kernel(tc, x, z, W, b, out):
             for mm in range(2):
                 for u in range(2):
                     nc.tensor.transpose(w_t[:, mm, u, :], w_words[:, 2 * mp + mm, u, :], ident[:])
+            nc.vector.quantize_mx(
+                out=u_codes[:, mp * N_PASS : (mp + 1) * N_PASS].bitcast(FP8X4),
+                scales=u_scales[:, mp * N_PASS : (mp + 1) * N_PASS],
+                in_=u_bf[:, mp * N_PASS * PACK : (mp + 1) * N_PASS * PACK],
+            )
             nc.vector.tensor_copy(
                 out=w_bf_words[:, 2 * mp : 2 * mp + 2, :, :],
                 in_=w_t[:].rearrange("q mm u p -> q mm p u"),
             )
-
-        for h in range(2):
-            nc.vector.quantize_mx(
-                out=u_codes[:, h * N_PASS : (h + 1) * N_PASS].bitcast(FP8X4),
-                scales=u_scales[:, h * N_PASS : (h + 1) * N_PASS],
-                in_=u_bf[:, h * N_PASS * PACK : (h + 1) * N_PASS * PACK],
-            )
-        nc.vector.quantize_mx(out=w_codes[:].bitcast(FP8X4), scales=w_scales[:], in_=w_bf[:])
-
         bias = keep.tile([P, GROUPS], F32)
         nc.vector.tensor_copy(out=bias[:], in_=b_sb[:])
+        nc.vector.quantize_mx(out=w_codes[:].bitcast(FP8X4), scales=w_scales[:], in_=w_bf[:])
 
         y_sb = keep.tile([P, GROUPS, Y_POS], F32)
         y_view = y_sb[:].rearrange(
@@ -113,10 +112,8 @@ def tile_upconvcropcat_kernel(tc, x, z, W, b, out):
                 .rearrange("p (d r) -> p d r", d=YD)[:, :, 0 : YH * ZW]
                 .rearrange("p d (h w) -> p d h w", h=YH)[:, :, :, 0:YW],
             )
-            if g == 0:
-                nc.sync.dma_start(out=zc_dram[:, 0, :], in_=zc_sb[:, 0, :])
-            if g == GROUPS - 1:
-                nc.sync.dma_start(out=zc_dram[:, 1:GROUPS, :], in_=zc_sb[:, 1:GROUPS, :])
+            if g % 2 == 1:
+                nc.sync.dma_start(out=zc_dram[:, g - 1 : g + 1, :], in_=zc_sb[:, g - 1 : g + 1, :])
 
             m = g
             for ip in range(2):
@@ -132,20 +129,12 @@ def tile_upconvcropcat_kernel(tc, x, z, W, b, out):
                             start=True,
                             stop=True,
                         )
-                        if m < GROUPS - 1:
-                            nc.scalar.activation(
-                                out=y_view[:, m, ip, :, di, :, dj, :],
-                                in_=acc[:].rearrange("p (ii j k) -> p ii j k", ii=2, j=XH),
-                                func=mybir.ActivationFunctionType.Identity,
-                                bias=bias[:, m : m + 1],
-                                scale=1.0,
-                            )
-                        else:
-                            nc.vector.tensor_scalar(
-                                out=y_view[:, m, ip, :, di, :, dj, :],
-                                in0=acc[:].rearrange("p (ii j k) -> p ii j k", ii=2, j=XH),
-                                scalar1=bias[:, m : m + 1],
-                                scalar2=None,
-                                op0=mybir.AluOpType.add,
-                            )
-        nc.sync.dma_start(out=y_dram, in_=y_sb[:])
+                        nc.scalar.activation(
+                            out=y_view[:, m, ip, :, di, :, dj, :],
+                            in_=acc[:].rearrange("p (ii j k) -> p ii j k", ii=2, j=XH),
+                            func=mybir.ActivationFunctionType.Identity,
+                            bias=bias[:, m : m + 1],
+                            scale=1.0,
+                        )
+            if m % 2 == 1:
+                nc.scalar.dma_start(out=y_dram[:, m - 1 : m + 1, :], in_=y_sb[:, m - 1 : m + 1, :])

@@ -49,14 +49,13 @@ def tile_upconvcropcat_kernel(tc, x, z, W, b, out):
         x_sb = keep.tile([P, PACK, X_POS], BF16)
         nc.sync.dma_start(out=x_sb[:], in_=x[0].rearrange("(p t) d h w -> p t (d h w)", t=PACK))
         w_sb = keep.tile([P, GROUPS * C], BF16)
-        nc.scalar.dma_start(out=w_sb[:], in_=W.rearrange("(p m) c -> p (m c)", m=GROUPS))
+        nc.sync.dma_start(out=w_sb[:], in_=W.rearrange("(p m) c -> p (m c)", m=GROUPS))
         b_sb = keep.tile([P, GROUPS], BF16)
         nc.scalar.dma_start(out=b_sb[:], in_=b.rearrange("(p m) -> p m", m=GROUPS))
         z_in = []
         for g in range(GROUPS):
             z_g = keep.tile([P, Z_SKIP + YD * ZH * ZW], BF16, name="z_in%d" % g)
-            queue = nc.sync if g % 2 == 0 else nc.scalar
-            queue.dma_start(out=z_g[:, 0 : Z_HI - Z_LO], in_=z_dram[:, g, Z_LO:Z_HI])
+            nc.sync.dma_start(out=z_g[:, 0 : Z_HI - Z_LO], in_=z_dram[:, g, Z_LO:Z_HI])
             z_in.append(z_g)
 
         ident = keep.tile([P, P], F32)
@@ -96,6 +95,18 @@ def tile_upconvcropcat_kernel(tc, x, z, W, b, out):
                 out=w_bf_words[:, 2 * mp : 2 * mp + 2, :, :],
                 in_=w_t[:].rearrange("q mm u p -> q mm p u"),
             )
+        zc_sb = keep.tile([P, GROUPS, Y_POS], F32)
+
+        def cast_z(g):
+            nc.vector.tensor_copy(
+                out=zc_sb[:, g, :].rearrange("p (d h w) -> p d h w", d=YD, h=YH),
+                in_=z_in[g][:, Z_SKIP : Z_SKIP + YD * ZH * ZW]
+                .rearrange("p (d r) -> p d r", d=YD)[:, :, 0 : YH * ZW]
+                .rearrange("p d (h w) -> p d h w", h=YH)[:, :, :, 0:YW],
+            )
+
+        cast_z(0)
+        nc.sync.dma_start(out=zc_dram[:, 0, :], in_=zc_sb[:, 0, :])
         bias = keep.tile([P, GROUPS], F32)
         nc.vector.tensor_copy(out=bias[:], in_=b_sb[:])
         nc.vector.quantize_mx(out=w_codes[:].bitcast(FP8X4), scales=w_scales[:], in_=w_bf[:])
@@ -104,16 +115,13 @@ def tile_upconvcropcat_kernel(tc, x, z, W, b, out):
         y_view = y_sb[:].rearrange(
             "p m (ip ii di j dj k) -> p m ip ii di j dj k", ip=2, ii=2, di=2, j=XH, dj=2
         )
-        zc_sb = keep.tile([P, GROUPS, Y_POS], F32)
         for g in range(GROUPS):
-            nc.vector.tensor_copy(
-                out=zc_sb[:, g, :].rearrange("p (d h w) -> p d h w", d=YD, h=YH),
-                in_=z_in[g][:, Z_SKIP : Z_SKIP + YD * ZH * ZW]
-                .rearrange("p (d r) -> p d r", d=YD)[:, :, 0 : YH * ZW]
-                .rearrange("p d (h w) -> p d h w", h=YH)[:, :, :, 0:YW],
-            )
-            if g % 2 == 1:
-                nc.sync.dma_start(out=zc_dram[:, g - 1 : g + 1, :], in_=zc_sb[:, g - 1 : g + 1, :])
+            if g > 0:
+                cast_z(g)
+            if g == 1:
+                nc.sync.dma_start(out=zc_dram[:, 1, :], in_=zc_sb[:, 1, :])
+            if g == 3:
+                nc.sync.dma_start(out=zc_dram[:, 2:4, :], in_=zc_sb[:, 2:4, :])
 
             m = g
             for ip in range(2):

@@ -50,8 +50,11 @@ def tile_upconvcropcat_kernel(tc, x, z, W, b, out):
         nc.sync.dma_start(out=x_sb[:], in_=x[0].rearrange("(p t) d h w -> p t (d h w)", t=PACK))
         w_sb = keep.tile([P, GROUPS * C], BF16)
         nc.sync.dma_start(out=w_sb[:], in_=W.rearrange("(p m) c -> p (m c)", m=GROUPS))
-        b_sb = keep.tile([P, GROUPS], BF16)
-        nc.scalar.dma_start(out=b_sb[:], in_=b.rearrange("(p m) -> p m", m=GROUPS))
+        b_row = keep.tile([P, O], BF16)
+        nc.vector.memset(b_row[:], 0.0)
+        ones = keep.tile([P, 1], BF16)
+        nc.vector.memset(ones[:], 1.0)
+        nc.scalar.dma_start(out=b_row[0:1, :], in_=b.rearrange("(a n) -> a n", a=1))
         z_in = []
         for g in range(GROUPS):
             z_g = keep.tile([P, Z_SKIP + YD * ZH * ZW], BF16, name="z_in%d" % g)
@@ -107,8 +110,12 @@ def tile_upconvcropcat_kernel(tc, x, z, W, b, out):
 
         cast_z(0)
         nc.sync.dma_start(out=zc_dram[:, 0, :], in_=zc_sb[:, 0, :])
+        bias_ps = psum_w.tile([P, GROUPS], F32, name="w_t")
+        b_cols = b_row[:].rearrange("k (p m) -> k m p", m=GROUPS)
+        for m in range(GROUPS):
+            nc.tensor.matmul(bias_ps[:, m : m + 1], lhsT=b_cols[:, m, :], rhs=ones[:], start=True, stop=True)
         bias = keep.tile([P, GROUPS], F32)
-        nc.vector.tensor_copy(out=bias[:], in_=b_sb[:])
+        nc.vector.tensor_copy(out=bias[:], in_=bias_ps[:])
         nc.vector.quantize_mx(out=w_codes[:].bitcast(FP8X4), scales=w_scales[:], in_=w_bf[:])
 
         y_sb = keep.tile([P, GROUPS, Y_POS], F32)

@@ -46,15 +46,15 @@ def tile_upconvcropcat_kernel(tc, x, z, W, b, out):
         zc_dram = out_rows[O : O + CZ, :].rearrange("(p g) n -> p g n", g=GROUPS)
         z_dram = z[0].rearrange("(p g) d h w -> p g (d h w)", g=GROUPS)
 
-        x_sb = keep.tile([P, PACK, X_POS], BF16)
-        nc.sync.dma_start(out=x_sb[:], in_=x[0].rearrange("(p t) d h w -> p t (d h w)", t=PACK))
-        w_sb = keep.tile([P, GROUPS * C], BF16)
-        nc.sync.dma_start(out=w_sb[:], in_=W.rearrange("(p m) c -> p (m c)", m=GROUPS))
         b_row = keep.tile([P, O], BF16)
         nc.vector.memset(b_row[:], 0.0)
         ones = keep.tile([P, 1], BF16)
         nc.vector.memset(ones[:], 1.0)
-        nc.scalar.dma_start(out=b_row[0:1, :], in_=b.rearrange("(a n) -> a n", a=1))
+        x_sb = keep.tile([P, PACK, X_POS], BF16)
+        nc.sync.dma_start(out=x_sb[:], in_=x[0].rearrange("(p t) d h w -> p t (d h w)", t=PACK))
+        w_sb = keep.tile([P, GROUPS * C], BF16)
+        nc.sync.dma_start(out=w_sb[:], in_=W.rearrange("(p m) c -> p (m c)", m=GROUPS))
+        nc.sync.dma_start(out=b_row[0:1, :], in_=b.rearrange("(a n) -> a n", a=1))
         z_in = []
         for g in range(GROUPS):
             z_g = keep.tile([P, Z_SKIP + YD * ZH * ZW], BF16, name="z_in%d" % g)
@@ -108,8 +108,6 @@ def tile_upconvcropcat_kernel(tc, x, z, W, b, out):
                 .rearrange("p d (h w) -> p d h w", h=YH)[:, :, :, 0:YW],
             )
 
-        cast_z(0)
-        nc.sync.dma_start(out=zc_dram[:, 0, :], in_=zc_sb[:, 0, :])
         bias_ps = psum_w.tile([P, GROUPS], F32, name="w_t")
         b_cols = b_row[:].rearrange("k (p m) -> k m p", m=GROUPS)
         for m in range(GROUPS):
@@ -122,15 +120,11 @@ def tile_upconvcropcat_kernel(tc, x, z, W, b, out):
         y_view = y_sb[:].rearrange(
             "p m (ip ii di j dj k) -> p m ip ii di j dj k", ip=2, ii=2, di=2, j=XH, dj=2
         )
-        for g in range(GROUPS):
-            if g > 0:
-                cast_z(g)
-            if g == 1:
-                nc.sync.dma_start(out=zc_dram[:, 1, :], in_=zc_sb[:, 1, :])
-            if g == 3:
-                nc.sync.dma_start(out=zc_dram[:, 2:4, :], in_=zc_sb[:, 2:4, :])
+        for m in range(GROUPS):
+            cast_z(m)
+            if m % 2 == 1:
+                nc.sync.dma_start(out=zc_dram[:, m - 1 : m + 1, :], in_=zc_sb[:, m - 1 : m + 1, :])
 
-            m = g
             for ip in range(2):
                 for di in range(2):
                     for dj in range(2):
@@ -151,5 +145,4 @@ def tile_upconvcropcat_kernel(tc, x, z, W, b, out):
                             bias=bias[:, m : m + 1],
                             scale=1.0,
                         )
-            if m % 2 == 1:
-                nc.scalar.dma_start(out=y_dram[:, m - 1 : m + 1, :], in_=y_sb[:, m - 1 : m + 1, :])
+        nc.sync.dma_start(out=y_dram[:, :, :], in_=y_sb[:])

from contextlib import ExitStack

import concourse.mybir as mybir
from concourse.masks import make_identity

FP8X4 = mybir.dt.float8_e4m3fn_x4
BF16 = mybir.dt.bfloat16
F32 = mybir.dt.float32
U32 = mybir.dt.uint32
U8 = mybir.dt.uint8

P = 128
PACK = 4
C = 512
O = 512
CZ = 512
XD, XH, XW = 4, 8, 16
X_POS = XD * XH * XW
YD, YH, YW = 8, 16, 32
Y_POS = YD * YH * YW
ZH, ZW = 20, 36
MARGIN = 2
GROUPS = 4
Z_CH = 12 * ZH * ZW
Z_NEED_FIRST = (MARGIN * ZH + MARGIN) * ZW + MARGIN
Z_NEED_LAST = ((MARGIN + YD - 1) * ZH + MARGIN + YH - 1) * ZW + MARGIN + YW - 1
Z_LO = Z_NEED_FIRST // 32 * 32
Z_HI = (Z_NEED_LAST + 32) // 32 * 32
Z_SKIP = Z_NEED_FIRST - Z_LO
N_PASS = 512

FLOPS = 2 * O * C * Y_POS
BYTES = 2 * (C * X_POS + O * C + O + CZ * Y_POS) + 4 * (O + CZ) * Y_POS


def tile_upconvcropcat_kernel(tc, x, z, W, b, out):
    nc = tc.nc
    with ExitStack() as ctx:
        keep = ctx.enter_context(tc.tile_pool(name="keep", bufs=1))
        psum_w = ctx.enter_context(tc.psum_pool(name="psum_w", bufs=2))
        psum_y = ctx.enter_context(tc.psum_pool(name="psum_y", bufs=6))
        ctx.enter_context(tc.manual_schedule())

        out_rows = out[0].rearrange("c d h w -> c (d h w)")
        y_dram = out_rows[0:O, :].rearrange("(p m) n -> p m n", m=GROUPS)
        zc_dram = out_rows[O : O + CZ, :].rearrange("(p g) n -> p g n", g=GROUPS)
        z_dram = z[0].rearrange("(p g) d h w -> p g (d h w)", g=GROUPS)

        b_row = keep.tile([P, O], BF16)
        nc.vector.memset(b_row[:], 0.0)
        ones = keep.tile([P, 1], BF16)
        nc.vector.memset(ones[:], 1.0)
        x_sb = keep.tile([P, PACK, X_POS], BF16)
        nc.sync.dma_start(out=x_sb[:], in_=x[0].rearrange("(p t) d h w -> p t (d h w)", t=PACK))
        w_sb = keep.tile([P, GROUPS * C], BF16)
        nc.sync.dma_start(out=w_sb[:], in_=W.rearrange("(p m) c -> p (m c)", m=GROUPS))
        nc.sync.dma_start(out=b_row[0:1, :], in_=b.rearrange("(a n) -> a n", a=1))
        z_in = []
        for g in range(GROUPS):
            z_g = keep.tile([P, Z_SKIP + YD * ZH * ZW], BF16, name="z_in%d" % g)
            nc.sync.dma_start(out=z_g[:, 0 : Z_HI - Z_LO], in_=z_dram[:, g, Z_LO:Z_HI])
            z_in.append(z_g)

        ident = keep.tile([P, P], F32)
        make_identity(nc, ident[:])

        u_bf = keep.tile([P, 2 * X_POS * PACK], BF16, align_bytes=64)
        u_codes = keep.tile([P, 2 * X_POS], U32, align_bytes=64)
        u_scales = keep.tile([P, 2 * X_POS], U8, align_bytes=64)
        half_pos = X_POS // 2
        for h in range(2):
            nc.vector.tensor_copy(
                out=u_bf[:, h * N_PASS * PACK : (h + 1) * N_PASS * PACK].rearrange(
                    "p (n r t) -> p n r t", r=2, t=PACK
                ),
                in_=x_sb[:, :, h * half_pos : (h + 1) * half_pos]
                .rearrange("p t n -> p n t")
                .unsqueeze(2)
                .to_broadcast([P, half_pos, 2, PACK]),
            )

        w_words = w_sb[:].bitcast(F32).rearrange("p (m q u) -> p m u q", m=GROUPS, u=2)
        w_bf = keep.tile([P, GROUPS * P * PACK], BF16, align_bytes=64)
        w_bf_words = w_bf[:].bitcast(F32).rearrange("q (m p u) -> q m p u", m=GROUPS, u=2)
        w_codes = keep.tile([P, GROUPS * P], U32, align_bytes=64)
        w_scales = keep.tile([P, GROUPS * P], U8, align_bytes=64)
        for mp in range(2):
            w_t = psum_w.tile([P, 2, 2, P], F32, name="w_t")
            for mm in range(2):
                for u in range(2):
                    nc.tensor.transpose(w_t[:, mm, u, :], w_words[:, 2 * mp + mm, u, :], ident[:])
            nc.vector.quantize_mx(
                out=u_codes[:, mp * N_PASS : (mp + 1) * N_PASS].bitcast(FP8X4),
                scales=u_scales[:, mp * N_PASS : (mp + 1) * N_PASS],
                in_=u_bf[:, mp * N_PASS * PACK : (mp + 1) * N_PASS * PACK],
            )
            nc.vector.tensor_copy(
                out=w_bf_words[:, 2 * mp : 2 * mp + 2, :, :],
                in_=w_t[:].rearrange("q mm u p -> q mm p u"),
            )
        zc_sb = keep.tile([P, GROUPS, Y_POS], F32)

        def cast_z(g):
            nc.vector.tensor_copy(
                out=zc_sb[:, g, :].rearrange("p (d h w) -> p d h w", d=YD, h=YH),
                in_=z_in[g][:, Z_SKIP : Z_SKIP + YD * ZH * ZW]
                .rearrange("p (d r) -> p d r", d=YD)[:, :, 0 : YH * ZW]
                .rearrange("p d (h w) -> p d h w", h=YH)[:, :, :, 0:YW],
            )

        bias_ps = psum_w.tile([P, GROUPS], F32, name="w_t")
        b_cols = b_row[:].rearrange("k (p m) -> k m p", m=GROUPS)
        for m in range(GROUPS):
            nc.tensor.matmul(bias_ps[:, m : m + 1], lhsT=b_cols[:, m, :], rhs=ones[:], start=True, stop=True)
        bias = keep.tile([P, GROUPS], F32)
        nc.vector.tensor_copy(out=bias[:], in_=bias_ps[:])
        nc.vector.quantize_mx(out=w_codes[:].bitcast(FP8X4), scales=w_scales[:], in_=w_bf[:])

        y_sb = keep.tile([P, GROUPS, Y_POS], F32)
        y_view = y_sb[:].rearrange(
            "p m (ip ii di j dj k) -> p m ip ii di j dj k", ip=2, ii=2, di=2, j=XH, dj=2
        )
        for m in range(GROUPS):
            cast_z(m)
            if m % 2 == 1:
                nc.sync.dma_start(out=zc_dram[:, m - 1 : m + 1, :], in_=zc_sb[:, m - 1 : m + 1, :])

            for ip in range(2):
                for di in range(2):
                    for dj in range(2):
                        acc = psum_y.tile([P, N_PASS], F32, name="acc")
                        nc.tensor.matmul_mx(
                            out=acc[:],
                            lhsT=w_codes[:, m * P : (m + 1) * P].bitcast(FP8X4),
                            lhsT_scale=w_scales[:, m * P : (m + 1) * P],
                            rhs=u_codes[:, ip * N_PASS : (ip + 1) * N_PASS].bitcast(FP8X4),
                            rhs_scale=u_scales[:, ip * N_PASS : (ip + 1) * N_PASS],
                            start=True,
                            stop=True,
                        )
                        nc.scalar.activation(
                            out=y_view[:, m, ip, :, di, :, dj, :],
                            in_=acc[:].rearrange("p (ii j k) -> p ii j k", ii=2, j=XH),
                            func=mybir.ActivationFunctionType.Identity,
                            bias=bias[:, m : m + 1],
                            scale=1.0,
                        )
        nc.sync.dma_start(out=y_dram[:, :, :], in_=y_sb[:])
